import numpy as np
import ml_dtypes


def mxq(x, axis, fmt="e4m3"):
    dtype, down = {"e4m3": (ml_dtypes.float8_e4m3fn, 7), "e5m2": (ml_dtypes.float8_e5m2, 14)}[fmt]
    v = np.moveaxis(np.asarray(x, np.float32).astype(ml_dtypes.bfloat16).astype(np.float64), axis, -1)
    blocks = v.reshape(v.shape[:-1] + (-1, 32))
    amax = np.abs(blocks).max(-1, keepdims=True)
    byte = np.maximum(np.where(amax > 0, np.frexp(amax)[1] - 1 + 127, 0) - down, 1)
    scale = np.exp2(byte - 127.0)
    codes = (blocks / scale).astype(np.float32).astype(dtype).astype(np.float64)
    return np.moveaxis((codes * scale).reshape(v.shape), -1, axis)


WIDE = False


def mx_kscale(k):
    if not WIDE:
        return np.ones(k)
    levels = np.array([30, -30])
    if k % 512:
        return np.exp2(np.random.permutation(np.resize(levels, k // 32))).repeat(32)
    a = np.empty((k // 512, 16))
    for p in range(k // 512):
        a[p, :8] = np.random.permutation(np.resize(levels, 8))
        for g in range(8):
            far = levels[np.abs(levels - a[p, g]) >= 10]
            a[p, g + 8] = far[np.random.randint(len(far))]
    return np.exp2(a.ravel()).repeat(32)


BF16 = ml_dtypes.bfloat16


def bf(x):
    return np.asarray(x, np.float32).astype(BF16)


def f64(x):
    return np.asarray(x).astype(np.float64)


B, N, D = 4, 512, 512
C = 2 * D
EPS_BN = 1e-5
NEG_SLOPE = 0.01


def bn_lrelu(x, g, b):
    mean = np.mean(x, axis=(0, 2), keepdims=True)
    var = np.var(x, axis=(0, 2), keepdims=True)
    y = (x - mean) / np.sqrt(var + EPS_BN) * g[None, :, None] + b[None, :, None]
    return np.where(y >= 0, y, NEG_SLOPE * y)


def setup_inputs():
    s = mx_kscale(C)
    v = np.random.standard_normal((B, C, N))
    return {"h1": bf(np.where(v >= 0, v, NEG_SLOPE * v) * s[None, :, None]),
            "W2": bf(np.random.standard_normal((D, C)) / np.sqrt(C) / s[None, :]),
            "g2": bf(1.0 + 0.2 * np.random.standard_normal(D)),
            "b2": bf(0.3 * np.random.standard_normal(D))}


def reference(h1, W2, g2, b2):
    z = mxq(f64(W2), 1, "e5m2") @ mxq(f64(h1), 1, "e5m2")
    return np.swapaxes(bn_lrelu(z, f64(g2), f64(b2)), 1, 2)

@@ -1,0 +1,398 @@
+from contextlib import ExitStack
+
+import concourse.mybir as mybir
+from concourse.masks import make_identity
+
+B, N, D = 4, 512, 512
+C = 2 * D
+EPS_BN = 1e-5
+NEG_SLOPE = 0.01
+FLOPS = 2 * B * N * D * C
+
+F32 = mybir.dt.float32
+BF16 = mybir.dt.bfloat16
+U32 = mybir.dt.uint32
+U8 = mybir.dt.uint8
+E5M2X4 = mybir.dt.float8_e5m2_x4
+ALU = mybir.AluOpType
+ACT = mybir.ActivationFunctionType
+
+P = 128
+PACK = 4
+K_PASS = P * PACK
+PASSES = C // K_PASS
+CHUNKS = B * PASSES
+O_TILES = D // P
+N_TILES = N // P
+RUN = 4
+VECTOR_NODES = 224
+FIRST_VECTOR_NODES = 424
+LATE = 9
+LATE_NODES = 512
+W_BANK = [6,7,6,2]
+Z_BANK = [[0,1,2,3],[4,5,6,7],[4,5,6,7],[7,3,2,3]]
+T_BANK = [[0,1,0,1],[0,1,0,1],[4,5,6,7],[4,5,2,3]]
+
+
+def tile_yuyipointupdate_pb_kernel(tc, h1, W2, g2, b2, out):
+    nc = tc.nc
+
+    with ExitStack() as ctx:
+        keep = ctx.enter_context(tc.tile_pool(name="keep", bufs=1))
+        stage = ctx.enter_context(tc.tile_pool(name="stage", bufs=3))
+        post = ctx.enter_context(tc.tile_pool(name="post", bufs=6))
+        psum = ctx.enter_context(tc.psum_pool(name="psum", bufs=1))
+
+        ident = keep.tile([P, P], F32)
+        ident_bf16 = keep.tile([P, P], BF16)
+        gb_rows = keep.tile([P, P], BF16)
+        gb_cols = keep.tile([P, 3, O_TILES], F32)
+        minus_half = keep.tile([P, 1], F32)
+        h_raw = keep.tile([P, CHUNKS, PACK, N], BF16)
+        w_raw = keep.tile([P, O_TILES, C], BF16)
+        h_codes = keep.tile([P, CHUNKS, N], U32, align_bytes=64)
+        h_scales = keep.tile([P, CHUNKS, N], U8, align_bytes=64)
+        w_codes = keep.tile([P, O_TILES, PASSES * P], U32, align_bytes=64)
+        w_scales = keep.tile([P, O_TILES, PASSES * P], U8, align_bytes=64)
+        stats = keep.tile([P, O_TILES, B * 6], F32)
+        mean_var = keep.tile([P, O_TILES, 2], F32)
+        std = keep.tile([P, O_TILES], F32)
+        rstd = keep.tile([P, O_TILES], F32)
+        gain = keep.tile([P, O_TILES, 2], F32)
+        shift = keep.tile([P, O_TILES], F32)
+
+        make_identity(nc, ident[:])
+        nc.gpsimd.memset(gb_rows[:], 0.0)
+        nc.gpsimd.memset(minus_half[:], -0.5)
+        nc.scalar.activation(out=ident_bf16[:], in_=ident[:], func=ACT.Copy)
+
+        def load_h(i, nodes):
+            b, g = divmod(i, PASSES)
+            rows = h1[b, g * K_PASS : (g + 1) * K_PASS, nodes]
+            nc.sync.dma_start(out=h_raw[:, i, :, nodes], in_=rows.rearrange("(p t) n -> p t n", t=PACK))
+
+        def load_w(j):
+            nc.sync.dma_start(out=w_raw[:, j, :], in_=W2[j * P : (j + 1) * P, :])
+
+        all_nodes = slice(0, N)
+        vector_nodes = slice(0, N // 2)
+        scalar_nodes = slice(N // 2, N)
+        load_w(0)
+        load_h(0, vector_nodes)
+        load_h(0, scalar_nodes)
+        load_h(1, all_nodes)
+        load_h(2, all_nodes)
+        load_w(1)
+        nc.sync.dma_start(out=gb_rows[0:O_TILES, :], in_=g2.rearrange("(j p) -> j p", p=P))
+        nc.sync.dma_start(out=gb_rows[O_TILES : 2 * O_TILES, :], in_=b2.rearrange("(j p) -> j p", p=P))
+        load_h(3, all_nodes)
+        load_h(4, all_nodes)
+        load_w(3)
+        load_h(5, all_nodes)
+        load_w(2)
+        load_h(6, all_nodes)
+        load_h(7, all_nodes)
+
+        def bank_tile(bank, shape, dtype):
+            return psum.tile(shape, dtype, name="bank%d" % bank, tag="bank%d" % bank)
+
+        h_grouped, w_ts, w_grouped, z, y, r, r_t = {}, {}, {}, {}, {}, {}, {}
+
+        extra = {}
+
+        def interleave_h(i):
+            h_grouped[i] = stage.tile([P, N, PACK], BF16, name="h_grouped", align_bytes=64)
+            split = FIRST_VECTOR_NODES if i == 0 else (VECTOR_NODES if i < LATE else LATE_NODES)
+            pieces = [(nc.vector.tensor_copy, slice(0, split))] + ([(nc.scalar.copy, slice(split, N))] if split < N else [])
+            if i == 0:
+                pieces = [(nc.vector.tensor_copy, slice(0, N // 2)), (nc.vector.tensor_copy, slice(N // 2, split))] + pieces[1:]
+            for copy, nodes in pieces:
+                copy(
+                    out=h_grouped[i][:, nodes, :].rearrange("p (c i) t -> p c t i", i=RUN),
+                    in_=h_raw[:, i, :, nodes].rearrange("p t (c i) -> p c t i", i=RUN),
+                )
+
+        def quantize_h(i):
+            nc.vector.quantize_mx(
+                out=h_codes[:, i, :].bitcast(E5M2X4),
+                scales=h_scales[:, i, :],
+                in_=h_grouped[i][:].rearrange("p n t -> p (n t)"),
+            )
+
+        def transpose_w(j):
+            words = w_raw[:, j, :].bitcast(F32)
+            w_t = bank_tile(W_BANK[j], [P, 2 * PASSES, P], F32)
+            half = K_PASS // 2
+            for g in range(PASSES):
+                for u in range(2):
+                    nc.tensor.transpose(w_t[:, 2 * g + u, :], words[:, half * g + u : half * (g + 1) : 2], ident[:])
+            w_ts[j] = w_t
+
+        def group_w(j):
+            w_grouped[j] = stage.tile([P, C], BF16, name="w_grouped", bufs=4, align_bytes=64)
+            nc.scalar.copy(
+                out=w_grouped[j][:].bitcast(F32).rearrange("p (g o u) -> p g o u", g=PASSES, u=2),
+                in_=w_ts[j][:].rearrange("p (g u) o -> p g o u", u=2),
+            )
+
+        def quantize_w(j):
+            nc.vector.quantize_mx(out=w_codes[:, j, :].bitcast(E5M2X4), scales=w_scales[:, j, :], in_=w_grouped[j][:])
+
+        def spread_gain_and_shift():
+            gb_t = bank_tile(3, [P, P], BF16)
+            nc.tensor.transpose(gb_t[:], gb_rows[:], ident_bf16[:])
+            nc.vector.tensor_copy(out=gb_cols[:, 0:2, :].rearrange("p a j -> p (a j)"), in_=gb_t[:, 0 : 2 * O_TILES])
+            nc.vector.tensor_scalar_mul(out=gb_cols[:, 2, :], in0=gb_t[:, 0:O_TILES], scalar1=-1.0)
+
+        def matmul_pass(j, b, g):
+            if g == 0:
+                z[j, b] = bank_tile(Z_BANK[j][b], [P, N], F32)
+            cols = slice(g * P, (g + 1) * P)
+            nc.tensor.matmul_mx(
+                out=z[j, b][:],
+                lhsT=w_codes[:, j, cols].bitcast(E5M2X4),
+                lhsT_scale=w_scales[:, j, cols],
+                rhs=h_codes[:, PASSES * b + g, :].bitcast(E5M2X4),
+                rhs_scale=h_scales[:, PASSES * b + g, :],
+                start=(g == 0),
+                stop=(g == PASSES - 1),
+            )
+
+        def matmul(j, b):
+            if j < O_TILES:
+                for g in range(PASSES):
+                    matmul_pass(j, b, g)
+
+        def statistics(j, b):
+            if j < O_TILES:
+                nc.vector.bn_stats(out=stats[:, j, 6 * b : 6 * (b + 1)], in_=z[j, b][:])
+
+        def deviation(j):
+            if j < O_TILES:
+                nc.vector.bn_aggr(out=mean_var[:, j, :], in_=stats[:, j, :])
+                nc.gpsimd.tensor_scalar(
+                    out=std[:, j : j + 1], in0=mean_var[:, j, 1:2], scalar1=EPS_BN, scalar2=1.0, op0=ALU.add, op1=ALU.mult
+                )
+
+        def invert(j):
+            if j < O_TILES:
+                nc.gpsimd.tensor_tensor(out=rstd[:, j : j + 1], in0=std[:, j : j + 1], in1=minus_half[:], op=ALU.pow)
+
+        def make_gain(j):
+            if j < O_TILES:
+                nc.scalar.activation(out=gain[:, j, :], in_=gb_cols[:, 0:3:2, j], func=ACT.Identity, scale=rstd[:, j : j + 1])
+
+        def make_shift(j):
+            if j < O_TILES:
+                nc.scalar.activation(
+                    out=shift[:, j : j + 1], in_=mean_var[:, j, 0:1], func=ACT.Identity,
+                    scale=gain[:, j, 1:2], bias=gb_cols[:, 1, j : j + 1],
+                )
+
+        def normalise(j, b):
+            y[j, b] = post.tile([P, N], F32, name="y")
+            nc.scalar.activation(
+                out=y[j, b][:], in_=z[j, b][:], func=ACT.Identity, scale=gain[:, j, 0:1], bias=shift[:, j : j + 1]
+            )
+
+        def park(j, b):
+            parked = keep.tile([P, N], F32, name="parked_%d_%d" % (j, b))
+            nc.scalar.copy(out=parked[:], in_=z[j, b][:])
+            z[j, b] = parked
+
+        def park_stats(j, b):
+            parked = keep.tile([P, N], F32, name="parked_%d_%d" % (j, b))
+            total = post.tile([P, 1], F32, name="total")
+            junk = post.tile([P, N], BF16, name="junk", bufs=2)
+            nc.scalar.activation(out=parked[:], in_=z[j, b][:], func=ACT.Identity, accum_out=total[:])
+            nc.scalar.activation(out=stats[:, j, 6 * b + 1 : 6 * b + 2], in_=total[:], func=ACT.Identity)
+            for a in range(2):
+                nc.scalar.activation(out=junk[:, a * 256 : (a + 1) * 256], in_=parked[:, a * 256 : (a + 1) * 256], func=ACT.Square, bias=stats[:, j, 6 * b + 1 : 6 * b + 2], accum_out=stats[:, j, 6 * b + 3 * a + 2 : 6 * b + 3 * a + 3])
+            z[j, b] = parked
+
+        def split(j, b, on_vector):
+            u = post.tile([P, N], F32, name="y")
+            v = post.tile([P, N], F32, name="r")
+            for w in (u, v):
+                if on_vector:
+                    nc.vector.tensor_scalar(out=w[:], in0=z[j, b][:], scalar1=gain[:, j, 0:1], scalar2=shift[:, j : j + 1], op0=ALU.mult, op1=ALU.add)
+                else:
+                    nc.scalar.activation(out=w[:], in_=z[j, b][:], func=ACT.Identity, scale=gain[:, j, 0:1], bias=shift[:, j : j + 1])
+            r[j, b] = u
+            extra[j, b] = v
+
+        def normalise_parked(j, b):
+            y[j, b] = post.tile([P, N], F32, name="y")
+            nc.vector.tensor_scalar(
+                out=y[j, b][:], in0=z[j, b][:], scalar1=gain[:, j, 0:1], scalar2=shift[:, j : j + 1], op0=ALU.mult, op1=ALU.add
+            )
+
+        def leaky_relu(j, b):
+            r[j, b] = post.tile([P, N], F32, name="r")
+            nc.vector.scalar_tensor_tensor(
+                out=r[j, b][:], in0=y[j, b][:], scalar=NEG_SLOPE, in1=y[j, b][:], op0=ALU.mult, op1=ALU.max
+            )
+
+        def transpose_r(j, b):
+            r_t[j, b] = bank_tile(T_BANK[j][b], [P, N_TILES, P], F32)
+            for t in range(N_TILES):
+                nc.tensor.transpose(r_t[j, b][:, t, :], r[j, b][:, t * P : (t + 1) * P], ident[:])
+                if (j, b) in extra:
+                    nc.tensor.transpose(r_t[j, b][:, t, :], extra[j, b][:, t * P : (t + 1) * P], ident[:])
+
+        def store(j, b, copy=nc.scalar.copy):
+            rows = post.tile([P, N_TILES, P], F32, name="rows", bufs=8)
+            copy(out=rows[:], in_=r_t[j, b][:])
+            nc.sync.dma_start(out=out[b, :, j * P : (j + 1) * P].rearrange("(t p) o -> p t o", p=P), in_=rows[:])
+
+        interleave_h(0)
+        interleave_h(1)
+        quantize_h(0)
+        transpose_w(0)
+        interleave_h(2)
+        quantize_h(1)
+        group_w(0)
+        transpose_w(1)
+        interleave_h(3)
+        quantize_h(2)
+        quantize_w(0)
+        group_w(1)
+        transpose_w(3)
+        matmul(0, 0)
+        matmul_pass(0, 1, 0)
+        spread_gain_and_shift()
+        interleave_h(4)
+        quantize_h(3)
+        quantize_w(1)
+        group_w(3)
+        transpose_w(2)
+        matmul_pass(0, 1, 1)
+        matmul(1, 0)
+        matmul(1, 1)
+        interleave_h(5)
+        quantize_h(4)
+        quantize_w(3)
+        group_w(2)
+        matmul(3, 0)
+        matmul_pass(0, 2, 0)
+        statistics(0, 0)
+        interleave_h(6)
+        quantize_h(5)
+        quantize_w(2)
+        park(3, 0)
+        matmul(3, 1)
+        matmul_pass(0, 2, 1)
+        matmul(1, 2)
+        statistics(0, 1)
+        interleave_h(7)
+        quantize_h(6)
+        park(3, 1)
+        matmul_pass(0, 3, 0)
+        statistics(0, 2)
+        matmul_pass(1, 3, 0)
+        quantize_h(7)
+        matmul_pass(0, 3, 1)
+        matmul_pass(1, 3, 1)
+        park(1, 0)
+        statistics(1, 0)
+        statistics(0, 3)
+        deviation(0)
+        invert(0)
+        park(1, 1)
+        matmul(2, 0)
+        make_gain(0)
+        make_shift(0)
+        statistics(1, 3)
+        statistics(1, 1)
+        park(1, 2)
+        matmul(2, 1)
+        statistics(1, 2)
+        deviation(1)
+        invert(1)
+        park(1, 3)
+        matmul(2, 2)
+        matmul(2, 3)
+        statistics(3, 0)
+        statistics(3, 1)
+        statistics(2, 0)
+        normalise(0, 0)
+        leaky_relu(0, 0)
+        transpose_r(0, 0)
+        normalise(0, 1)
+        make_gain(1)
+        leaky_relu(0, 1)
+        transpose_r(0, 1)
+        normalise(0, 2)
+        make_shift(1)
+        matmul(3, 2)
+        leaky_relu(0, 2)
+        normalise(0, 3)
+        matmul(3, 3)
+        leaky_relu(0, 3)
+        statistics(2, 1)
+        statistics(2, 2)
+        statistics(2, 3)
+        deviation(2)
+        invert(2)
+        store(0, 0)
+        transpose_r(0, 2)
+        store(0, 1)
+        transpose_r(0, 3)
+        normalise_parked(1, 0)
+        leaky_relu(1, 0)
+        make_gain(2)
+        store(0, 2)
+        transpose_r(1, 0)
+        make_shift(2)
+        store(0, 3)
+        statistics(3, 2)
+        statistics(3, 3)
+        deviation(3)
+        invert(3)
+        normalise(2, 0)
+        normalise_parked(1, 1)
+        leaky_relu(2, 0)
+        transpose_r(2, 0)
+        store(1, 0)
+        leaky_relu(1, 1)
+        transpose_r(1, 1)
+        normalise(2, 1)
+        make_gain(3)
+        normalise_parked(1, 2)
+        leaky_relu(2, 1)
+        transpose_r(2, 1)
+        make_shift(3)
+        store(2, 0)
+        leaky_relu(1, 2)
+        transpose_r(1, 2)
+        normalise(2, 2)
+        store(1, 1)
+        normalise_parked(1, 3)
+        leaky_relu(2, 2)
+        transpose_r(2, 2)
+        store(2, 1)
+        leaky_relu(1, 3)
+        transpose_r(1, 3)
+        normalise(2, 3)
+        store(1, 2)
+        normalise_parked(3, 0)
+        leaky_relu(2, 3)
+        transpose_r(2, 3)
+        store(2, 2)
+        leaky_relu(3, 0)
+        transpose_r(3, 0)
+        normalise(3, 2)
+        store(1, 3)
+        normalise_parked(3, 1)
+        leaky_relu(3, 2)
+        transpose_r(3, 2)
+        store(2, 3)
+        leaky_relu(3, 1)
+        transpose_r(3, 1)
+        normalise(3, 3)
+        store(3, 0)
+        leaky_relu(3, 3)
+        transpose_r(3, 3)
+        store(3, 2)
+        store(3, 1)
+        store(3, 3)

@@ -22,16 +22,28 @@ PACK = 4
 K_PASS = P * PACK
 PASSES = C // K_PASS
 CHUNKS = B * PASSES
-O_TILES = D // P
+GROUPS = D // P
 N_TILES = N // P
+TILES = GROUPS * B
+STATS = 6
 RUN = 4
-VECTOR_NODES = 224
+
+VECTOR_NODES = 232
 FIRST_VECTOR_NODES = 424
-LATE = 9
-LATE_NODES = 512
-W_BANK = [6,7,6,2]
-Z_BANK = [[0,1,2,3],[4,5,6,7],[4,5,6,7],[7,3,2,3]]
-T_BANK = [[0,1,0,1],[0,1,0,1],[4,5,6,7],[4,5,2,3]]
+
+PARKED = 2
+LEAD = 2
+LAG = 2
+
+
+def z_bank(j, b):
+    return {0: b, 1: B + b, PARKED: B + b, 3: LEAD + b}[j]
+
+
+def turned_bank(j, b):
+    if j == GROUPS - 1:
+        return z_bank(j, b)
+    return b % 2 if j == 0 or b < 2 else B + b
 
 
 def tile_yuyipointupdate_pb_kernel(tc, h1, W2, g2, b2, out):
@@ -46,27 +58,26 @@ def tile_yuyipointupdate_pb_kernel(tc, h1, W2, g2, b2, out):
         ident = keep.tile([P, P], F32)
         ident_bf16 = keep.tile([P, P], BF16)
         gb_rows = keep.tile([P, P], BF16)
-        gb_cols = keep.tile([P, 3, O_TILES], F32)
-        minus_half = keep.tile([P, 1], F32)
+        gb_cols = keep.tile([P, 3, GROUPS], F32)
         h_raw = keep.tile([P, CHUNKS, PACK, N], BF16)
-        w_raw = keep.tile([P, O_TILES, C], BF16)
+        w_raw = keep.tile([P, GROUPS, C], BF16)
         h_codes = keep.tile([P, CHUNKS, N], U32, align_bytes=64)
         h_scales = keep.tile([P, CHUNKS, N], U8, align_bytes=64)
-        w_codes = keep.tile([P, O_TILES, PASSES * P], U32, align_bytes=64)
-        w_scales = keep.tile([P, O_TILES, PASSES * P], U8, align_bytes=64)
-        stats = keep.tile([P, O_TILES, B * 6], F32)
-        mean_var = keep.tile([P, O_TILES, 2], F32)
-        std = keep.tile([P, O_TILES], F32)
-        rstd = keep.tile([P, O_TILES], F32)
-        gain = keep.tile([P, O_TILES, 2], F32)
-        shift = keep.tile([P, O_TILES], F32)
+        w_codes = keep.tile([P, GROUPS, PASSES * P], U32, align_bytes=64)
+        w_scales = keep.tile([P, GROUPS, PASSES * P], U8, align_bytes=64)
+        parked = keep.tile([P, B, N], F32)
+        stats = keep.tile([P, GROUPS, B * STATS], F32)
+        mean_var = keep.tile([P, GROUPS, 2], F32)
+        std = keep.tile([P, GROUPS], F32)
+        rstd = keep.tile([P, GROUPS], F32)
+        gain = keep.tile([P, GROUPS, 2], F32)
+        shift = keep.tile([P, GROUPS], F32)
 
         make_identity(nc, ident[:])
+        make_identity(nc, ident_bf16[:])
         nc.gpsimd.memset(gb_rows[:], 0.0)
-        nc.gpsimd.memset(minus_half[:], -0.5)
-        nc.scalar.activation(out=ident_bf16[:], in_=ident[:], func=ACT.Copy)
 
-        def load_h(i, nodes):
+        def load_h(i, nodes=slice(0, N)):
             b, g = divmod(i, PASSES)
             rows = h1[b, g * K_PASS : (g + 1) * K_PASS, nodes]
             nc.sync.dma_start(out=h_raw[:, i, :, nodes], in_=rows.rearrange("(p t) n -> p t n", t=PACK))
@@ -74,39 +85,36 @@ def tile_yuyipointupdate_pb_kernel(tc, h1, W2, g2, b2, out):
         def load_w(j):
             nc.sync.dma_start(out=w_raw[:, j, :], in_=W2[j * P : (j + 1) * P, :])
 
-        all_nodes = slice(0, N)
-        vector_nodes = slice(0, N // 2)
-        scalar_nodes = slice(N // 2, N)
         load_w(0)
-        load_h(0, vector_nodes)
-        load_h(0, scalar_nodes)
-        load_h(1, all_nodes)
-        load_h(2, all_nodes)
+        load_h(0, slice(0, N // 2))
+        load_h(0, slice(N // 2, N))
+        load_h(1)
+        load_h(2)
+        load_w(PARKED)
+        nc.sync.dma_start(out=gb_rows[0:GROUPS, :], in_=g2.rearrange("(j p) -> j p", p=P))
+        nc.sync.dma_start(out=gb_rows[GROUPS : 2 * GROUPS, :], in_=b2.rearrange("(j p) -> j p", p=P))
+        for i in range(3, CHUNKS - 1):
+            load_h(i)
         load_w(1)
-        nc.sync.dma_start(out=gb_rows[0:O_TILES, :], in_=g2.rearrange("(j p) -> j p", p=P))
-        nc.sync.dma_start(out=gb_rows[O_TILES : 2 * O_TILES, :], in_=b2.rearrange("(j p) -> j p", p=P))
-        load_h(3, all_nodes)
-        load_h(4, all_nodes)
+        load_h(CHUNKS - 1)
         load_w(3)
-        load_h(5, all_nodes)
-        load_w(2)
-        load_h(6, all_nodes)
-        load_h(7, all_nodes)
 
         def bank_tile(bank, shape, dtype):
             return psum.tile(shape, dtype, name="bank%d" % bank, tag="bank%d" % bank)
 
-        h_grouped, w_ts, w_grouped, z, y, r, r_t = {}, {}, {}, {}, {}, {}, {}
-
-        extra = {}
+        h_grouped, w_turned, w_grouped, z, y, r, r_turned = {}, {}, {}, {}, {}, {}, {}
 
         def interleave_h(i):
             h_grouped[i] = stage.tile([P, N, PACK], BF16, name="h_grouped", align_bytes=64)
-            split = FIRST_VECTOR_NODES if i == 0 else (VECTOR_NODES if i < LATE else LATE_NODES)
-            pieces = [(nc.vector.tensor_copy, slice(0, split))] + ([(nc.scalar.copy, slice(split, N))] if split < N else [])
             if i == 0:
-                pieces = [(nc.vector.tensor_copy, slice(0, N // 2)), (nc.vector.tensor_copy, slice(N // 2, split))] + pieces[1:]
-            for copy, nodes in pieces:
+                shares = [
+                    (nc.vector.tensor_copy, slice(0, N // 2)),
+                    (nc.vector.tensor_copy, slice(N // 2, FIRST_VECTOR_NODES)),
+                    (nc.scalar.copy, slice(FIRST_VECTOR_NODES, N)),
+                ]
+            else:
+                shares = [(nc.vector.tensor_copy, slice(0, VECTOR_NODES)), (nc.scalar.copy, slice(VECTOR_NODES, N))]
+            for copy, nodes in shares:
                 copy(
                     out=h_grouped[i][:, nodes, :].rearrange("p (c i) t -> p c t i", i=RUN),
                     in_=h_raw[:, i, :, nodes].rearrange("p t (c i) -> p c t i", i=RUN),
@@ -119,37 +127,36 @@ def tile_yuyipointupdate_pb_kernel(tc, h1, W2, g2, b2, out):
                 in_=h_grouped[i][:].rearrange("p n t -> p (n t)"),
             )
 
-        def transpose_w(j):
+        def turn_w(j):
             words = w_raw[:, j, :].bitcast(F32)
-            w_t = bank_tile(W_BANK[j], [P, 2 * PASSES, P], F32)
+            w_turned[j] = bank_tile(z_bank(PARKED, 2 + j // 2), [P, 2 * PASSES, P], F32)
             half = K_PASS // 2
             for g in range(PASSES):
                 for u in range(2):
-                    nc.tensor.transpose(w_t[:, 2 * g + u, :], words[:, half * g + u : half * (g + 1) : 2], ident[:])
-            w_ts[j] = w_t
+                    nc.tensor.transpose(w_turned[j][:, 2 * g + u, :], words[:, half * g + u : half * (g + 1) : 2], ident[:])
 
         def group_w(j):
-            w_grouped[j] = stage.tile([P, C], BF16, name="w_grouped", bufs=4, align_bytes=64)
+            w_grouped[j] = stage.tile([P, C], BF16, name="w_grouped", bufs=GROUPS, align_bytes=64)
             nc.scalar.copy(
                 out=w_grouped[j][:].bitcast(F32).rearrange("p (g o u) -> p g o u", g=PASSES, u=2),
-                in_=w_ts[j][:].rearrange("p (g u) o -> p g o u", u=2),
+                in_=w_turned[j][:].rearrange("p (g u) o -> p g o u", u=2),
             )
 
         def quantize_w(j):
             nc.vector.quantize_mx(out=w_codes[:, j, :].bitcast(E5M2X4), scales=w_scales[:, j, :], in_=w_grouped[j][:])
 
-        def spread_gain_and_shift():
-            gb_t = bank_tile(3, [P, P], BF16)
-            nc.tensor.transpose(gb_t[:], gb_rows[:], ident_bf16[:])
-            nc.vector.tensor_copy(out=gb_cols[:, 0:2, :].rearrange("p a j -> p (a j)"), in_=gb_t[:, 0 : 2 * O_TILES])
-            nc.vector.tensor_scalar_mul(out=gb_cols[:, 2, :], in0=gb_t[:, 0:O_TILES], scalar1=-1.0)
+        def turn_g2_b2():
+            gb_turned = bank_tile(z_bank(0, B - 1), [P, P], BF16)
+            nc.tensor.transpose(gb_turned[:], gb_rows[:], ident_bf16[:])
+            nc.vector.tensor_copy(out=gb_cols[:, 0:2, :].rearrange("p a j -> p (a j)"), in_=gb_turned[:, 0 : 2 * GROUPS])
+            nc.vector.tensor_scalar_mul(out=gb_cols[:, 2, :], in0=gb_turned[:, 0:GROUPS], scalar1=-1.0)
 
         def matmul_pass(j, b, g):
             if g == 0:
-                z[j, b] = bank_tile(Z_BANK[j][b], [P, N], F32)
+                z[j, b] = bank_tile(z_bank(j, b), [P, N], F32)[:]
             cols = slice(g * P, (g + 1) * P)
             nc.tensor.matmul_mx(
-                out=z[j, b][:],
+                out=z[j, b],
                 lhsT=w_codes[:, j, cols].bitcast(E5M2X4),
                 lhsT_scale=w_scales[:, j, cols],
                 rhs=h_codes[:, PASSES * b + g, :].bitcast(E5M2X4),
@@ -159,240 +166,155 @@ def tile_yuyipointupdate_pb_kernel(tc, h1, W2, g2, b2, out):
             )
 
         def matmul(j, b):
-            if j < O_TILES:
-                for g in range(PASSES):
-                    matmul_pass(j, b, g)
+            for g in range(PASSES):
+                matmul_pass(j, b, g)
+
+        def park(b):
+            nc.scalar.copy(out=parked[:, b, :], in_=z[PARKED, b])
+            z[PARKED, b] = parked[:, b, :]
 
         def statistics(j, b):
-            if j < O_TILES:
-                nc.vector.bn_stats(out=stats[:, j, 6 * b : 6 * (b + 1)], in_=z[j, b][:])
+            nc.vector.bn_stats(out=stats[:, j, STATS * b : STATS * (b + 1)], in_=z[j, b])
 
-        def deviation(j):
-            if j < O_TILES:
-                nc.vector.bn_aggr(out=mean_var[:, j, :], in_=stats[:, j, :])
-                nc.gpsimd.tensor_scalar(
-                    out=std[:, j : j + 1], in0=mean_var[:, j, 1:2], scalar1=EPS_BN, scalar2=1.0, op0=ALU.add, op1=ALU.mult
-                )
+        def make_std(j):
+            nc.vector.bn_aggr(out=mean_var[:, j, :], in_=stats[:, j, :])
+            nc.scalar.activation(out=std[:, j : j + 1], in_=mean_var[:, j, 1:2], func=ACT.Sqrt, bias=EPS_BN)
 
-        def invert(j):
-            if j < O_TILES:
-                nc.gpsimd.tensor_tensor(out=rstd[:, j : j + 1], in0=std[:, j : j + 1], in1=minus_half[:], op=ALU.pow)
+        def make_rstd(j):
+            nc.vector.reciprocal(out=rstd[:, j : j + 1], in_=std[:, j : j + 1])
 
         def make_gain(j):
-            if j < O_TILES:
-                nc.scalar.activation(out=gain[:, j, :], in_=gb_cols[:, 0:3:2, j], func=ACT.Identity, scale=rstd[:, j : j + 1])
+            nc.scalar.activation(out=gain[:, j, :], in_=gb_cols[:, 0:3:2, j], func=ACT.Identity, scale=rstd[:, j : j + 1])
 
         def make_shift(j):
-            if j < O_TILES:
-                nc.scalar.activation(
-                    out=shift[:, j : j + 1], in_=mean_var[:, j, 0:1], func=ACT.Identity,
-                    scale=gain[:, j, 1:2], bias=gb_cols[:, 1, j : j + 1],
-                )
-
-        def normalise(j, b):
-            y[j, b] = post.tile([P, N], F32, name="y")
             nc.scalar.activation(
-                out=y[j, b][:], in_=z[j, b][:], func=ACT.Identity, scale=gain[:, j, 0:1], bias=shift[:, j : j + 1]
+                out=shift[:, j : j + 1],
+                in_=mean_var[:, j, 0:1],
+                func=ACT.Identity,
+                scale=gain[:, j, 1:2],
+                bias=gb_cols[:, 1, j : j + 1],
             )
 
-        def park(j, b):
-            parked = keep.tile([P, N], F32, name="parked_%d_%d" % (j, b))
-            nc.scalar.copy(out=parked[:], in_=z[j, b][:])
-            z[j, b] = parked
+        def normalise_on_scalar(s):
+            j, b = divmod(s, B)
+            y[s] = post.tile([P, N], F32, name="y")
+            nc.scalar.activation(
+                out=y[s][:], in_=z[j, b], func=ACT.Identity, scale=gain[:, j, 0:1], bias=shift[:, j : j + 1]
+            )
 
-        def park_stats(j, b):
-            parked = keep.tile([P, N], F32, name="parked_%d_%d" % (j, b))
-            total = post.tile([P, 1], F32, name="total")
-            junk = post.tile([P, N], BF16, name="junk", bufs=2)
-            nc.scalar.activation(out=parked[:], in_=z[j, b][:], func=ACT.Identity, accum_out=total[:])
-            nc.scalar.activation(out=stats[:, j, 6 * b + 1 : 6 * b + 2], in_=total[:], func=ACT.Identity)
-            for a in range(2):
-                nc.scalar.activation(out=junk[:, a * 256 : (a + 1) * 256], in_=parked[:, a * 256 : (a + 1) * 256], func=ACT.Square, bias=stats[:, j, 6 * b + 1 : 6 * b + 2], accum_out=stats[:, j, 6 * b + 3 * a + 2 : 6 * b + 3 * a + 3])
-            z[j, b] = parked
-
-        def split(j, b, on_vector):
-            u = post.tile([P, N], F32, name="y")
-            v = post.tile([P, N], F32, name="r")
-            for w in (u, v):
-                if on_vector:
-                    nc.vector.tensor_scalar(out=w[:], in0=z[j, b][:], scalar1=gain[:, j, 0:1], scalar2=shift[:, j : j + 1], op0=ALU.mult, op1=ALU.add)
-                else:
-                    nc.scalar.activation(out=w[:], in_=z[j, b][:], func=ACT.Identity, scale=gain[:, j, 0:1], bias=shift[:, j : j + 1])
-            r[j, b] = u
-            extra[j, b] = v
-
-        def normalise_parked(j, b):
-            y[j, b] = post.tile([P, N], F32, name="y")
+        def normalise_on_vector(s):
+            j, b = divmod(s, B)
+            y[s] = post.tile([P, N], F32, name="y")
             nc.vector.tensor_scalar(
-                out=y[j, b][:], in0=z[j, b][:], scalar1=gain[:, j, 0:1], scalar2=shift[:, j : j + 1], op0=ALU.mult, op1=ALU.add
+                out=y[s][:], in0=z[j, b], scalar1=gain[:, j, 0:1], scalar2=shift[:, j : j + 1], op0=ALU.mult, op1=ALU.add
             )
 
-        def leaky_relu(j, b):
-            r[j, b] = post.tile([P, N], F32, name="r")
+        def leaky_relu(s):
+            r[s] = post.tile([P, N], F32, name="r")
             nc.vector.scalar_tensor_tensor(
-                out=r[j, b][:], in0=y[j, b][:], scalar=NEG_SLOPE, in1=y[j, b][:], op0=ALU.mult, op1=ALU.max
+                out=r[s][:], in0=y[s][:], scalar=NEG_SLOPE, in1=y[s][:], op0=ALU.mult, op1=ALU.max
             )
 
-        def transpose_r(j, b):
-            r_t[j, b] = bank_tile(T_BANK[j][b], [P, N_TILES, P], F32)
+        def turn_r(s):
+            r_turned[s] = bank_tile(turned_bank(*divmod(s, B)), [P, N_TILES, P], F32)
             for t in range(N_TILES):
-                nc.tensor.transpose(r_t[j, b][:, t, :], r[j, b][:, t * P : (t + 1) * P], ident[:])
-                if (j, b) in extra:
-                    nc.tensor.transpose(r_t[j, b][:, t, :], extra[j, b][:, t * P : (t + 1) * P], ident[:])
+                nc.tensor.transpose(r_turned[s][:, t, :], r[s][:, t * P : (t + 1) * P], ident[:])
 
-        def store(j, b, copy=nc.scalar.copy):
+        def store(s):
+            j, b = divmod(s, B)
             rows = post.tile([P, N_TILES, P], F32, name="rows", bufs=8)
-            copy(out=rows[:], in_=r_t[j, b][:])
+            nc.scalar.copy(out=rows[:], in_=r_turned[s][:])
             nc.sync.dma_start(out=out[b, :, j * P : (j + 1) * P].rearrange("(t p) o -> p t o", p=P), in_=rows[:])
 
+        turn_w(0)
         interleave_h(0)
+        group_w(0)
         interleave_h(1)
         quantize_h(0)
-        transpose_w(0)
+        quantize_w(0)
         interleave_h(2)
         quantize_h(1)
-        group_w(0)
-        transpose_w(1)
+        turn_w(PARKED)
+        group_w(PARKED)
+        turn_g2_b2()
+        matmul(0, 0)
         interleave_h(3)
         quantize_h(2)
-        quantize_w(0)
-        group_w(1)
-        transpose_w(3)
-        matmul(0, 0)
+        quantize_w(PARKED)
         matmul_pass(0, 1, 0)
-        spread_gain_and_shift()
+        statistics(0, 0)
         interleave_h(4)
         quantize_h(3)
-        quantize_w(1)
-        group_w(3)
-        transpose_w(2)
         matmul_pass(0, 1, 1)
-        matmul(1, 0)
-        matmul(1, 1)
+        matmul(PARKED, 0)
+        matmul(PARKED, 1)
         interleave_h(5)
         quantize_h(4)
-        quantize_w(3)
-        group_w(2)
-        matmul(3, 0)
+        turn_w(1)
         matmul_pass(0, 2, 0)
-        statistics(0, 0)
+        statistics(0, 1)
         interleave_h(6)
         quantize_h(5)
-        quantize_w(2)
-        park(3, 0)
-        matmul(3, 1)
+        turn_w(3)
         matmul_pass(0, 2, 1)
-        matmul(1, 2)
-        statistics(0, 1)
         interleave_h(7)
         quantize_h(6)
-        park(3, 1)
         matmul_pass(0, 3, 0)
         statistics(0, 2)
-        matmul_pass(1, 3, 0)
+        group_w(1)
+        group_w(3)
+        matmul(PARKED, 2)
         quantize_h(7)
         matmul_pass(0, 3, 1)
-        matmul_pass(1, 3, 1)
-        park(1, 0)
-        statistics(1, 0)
-        statistics(0, 3)
-        deviation(0)
-        invert(0)
-        park(1, 1)
-        matmul(2, 0)
-        make_gain(0)
-        make_shift(0)
-        statistics(1, 3)
-        statistics(1, 1)
-        park(1, 2)
-        matmul(2, 1)
-        statistics(1, 2)
-        deviation(1)
-        invert(1)
-        park(1, 3)
-        matmul(2, 2)
-        matmul(2, 3)
-        statistics(3, 0)
-        statistics(3, 1)
-        statistics(2, 0)
-        normalise(0, 0)
-        leaky_relu(0, 0)
-        transpose_r(0, 0)
-        normalise(0, 1)
-        make_gain(1)
-        leaky_relu(0, 1)
-        transpose_r(0, 1)
-        normalise(0, 2)
-        make_shift(1)
-        matmul(3, 2)
-        leaky_relu(0, 2)
-        normalise(0, 3)
-        matmul(3, 3)
-        leaky_relu(0, 3)
-        statistics(2, 1)
-        statistics(2, 2)
-        statistics(2, 3)
-        deviation(2)
-        invert(2)
-        store(0, 0)
-        transpose_r(0, 2)
-        store(0, 1)
-        transpose_r(0, 3)
-        normalise_parked(1, 0)
-        leaky_relu(1, 0)
-        make_gain(2)
-        store(0, 2)
-        transpose_r(1, 0)
-        make_shift(2)
-        store(0, 3)
-        statistics(3, 2)
-        statistics(3, 3)
-        deviation(3)
-        invert(3)
-        normalise(2, 0)
-        normalise_parked(1, 1)
-        leaky_relu(2, 0)
-        transpose_r(2, 0)
-        store(1, 0)
-        leaky_relu(1, 1)
-        transpose_r(1, 1)
-        normalise(2, 1)
-        make_gain(3)
-        normalise_parked(1, 2)
-        leaky_relu(2, 1)
-        transpose_r(2, 1)
-        make_shift(3)
-        store(2, 0)
-        leaky_relu(1, 2)
-        transpose_r(1, 2)
-        normalise(2, 2)
-        store(1, 1)
-        normalise_parked(1, 3)
-        leaky_relu(2, 2)
-        transpose_r(2, 2)
-        store(2, 1)
-        leaky_relu(1, 3)
-        transpose_r(1, 3)
-        normalise(2, 3)
-        store(1, 2)
-        normalise_parked(3, 0)
-        leaky_relu(2, 3)
-        transpose_r(2, 3)
-        store(2, 2)
-        leaky_relu(3, 0)
-        transpose_r(3, 0)
-        normalise(3, 2)
-        store(1, 3)
-        normalise_parked(3, 1)
-        leaky_relu(3, 2)
-        transpose_r(3, 2)
-        store(2, 3)
-        leaky_relu(3, 1)
-        transpose_r(3, 1)
-        normalise(3, 3)
-        store(3, 0)
-        leaky_relu(3, 3)
-        transpose_r(3, 3)
-        store(3, 2)
-        store(3, 1)
-        store(3, 3)
+        matmul(PARKED, 3)
+
+        engines = {mybir.EngineType.DVE, mybir.EngineType.Activation, mybir.EngineType.PE}
+        with tc.manual_schedule(engines=engines):
+            quantize_w(1)
+            quantize_w(3)
+            park(0)
+            park(1)
+            statistics(0, 3)
+            park(2)
+            make_std(0)
+            matmul(1, 0)
+            matmul(1, 1)
+            park(3)
+            statistics(1, 0)
+            make_rstd(0)
+            make_gain(0)
+            make_shift(0)
+            matmul(1, 2)
+            matmul(1, 3)
+            for b in range(1, B):
+                statistics(1, b)
+
+            on_vector = (10, 11, 13, 15)
+            stats_done = {0: 1, B: PARKED, 2 * B: 3}
+            for s in range(B - 1):
+                normalise_on_scalar(s)
+            for s in range(TILES + LAG):
+                if s + 1 in on_vector:
+                    normalise_on_vector(s + 1)
+                if s > LAG:
+                    store(s - LAG)
+                if s < TILES:
+                    leaky_relu(s)
+                    turn_r(s)
+                if s == 0:
+                    normalise_on_scalar(B - 1)
+                if s in stats_done:
+                    make_std(stats_done[s])
+                if s - 1 in stats_done:
+                    make_rstd(stats_done[s - 1])
+                    make_gain(stats_done[s - 1])
+                if s == 1:
+                    store(0)
+                if s - 1 in stats_done:
+                    make_shift(stats_done[s - 1])
+                if B <= s + LEAD < TILES and s + LEAD not in on_vector:
+                    normalise_on_scalar(s + LEAD)
+                if s < B:
+                    matmul(3, s)
+                if s < 2 * B:
+                    statistics(PARKED + s // B, s % B)

@@ -28,12 +28,14 @@ TILES = GROUPS * B
 STATS = 6
 RUN = 4
 
-VECTOR_NODES = 232
+VECTOR_NODES = 208
 FIRST_VECTOR_NODES = 424
 
 PARKED = 2
 LEAD = 2
 LAG = 2
+STATS_DONE = {0: 1, B: PARKED, 2 * B: 3}
+ON_VECTOR = (PARKED * B + 2, PARKED * B + 3, TILES - 3, TILES - 1)
 
 
 def z_bank(j, b):
@@ -68,7 +70,6 @@ def tile_yuyipointupdate_pb_kernel(tc, h1, W2, g2, b2, out):
         parked = keep.tile([P, B, N], F32)
         stats = keep.tile([P, GROUPS, B * STATS], F32)
         mean_var = keep.tile([P, GROUPS, 2], F32)
-        std = keep.tile([P, GROUPS], F32)
         rstd = keep.tile([P, GROUPS], F32)
         gain = keep.tile([P, GROUPS, 2], F32)
         shift = keep.tile([P, GROUPS], F32)
@@ -102,6 +103,7 @@ def tile_yuyipointupdate_pb_kernel(tc, h1, W2, g2, b2, out):
         def bank_tile(bank, shape, dtype):
             return psum.tile(shape, dtype, name="bank%d" % bank, tag="bank%d" % bank)
 
+        gb_turned = bank_tile(z_bank(0, B - 1), [P, P], BF16)
         h_grouped, w_turned, w_grouped, z, y, r, r_turned = {}, {}, {}, {}, {}, {}, {}
 
         def interleave_h(i):
@@ -146,8 +148,9 @@ def tile_yuyipointupdate_pb_kernel(tc, h1, W2, g2, b2, out):
             nc.vector.quantize_mx(out=w_codes[:, j, :].bitcast(E5M2X4), scales=w_scales[:, j, :], in_=w_grouped[j][:])
 
         def turn_g2_b2():
-            gb_turned = bank_tile(z_bank(0, B - 1), [P, P], BF16)
             nc.tensor.transpose(gb_turned[:], gb_rows[:], ident_bf16[:])
+
+        def spread_g2_b2():
             nc.vector.tensor_copy(out=gb_cols[:, 0:2, :].rearrange("p a j -> p (a j)"), in_=gb_turned[:, 0 : 2 * GROUPS])
             nc.vector.tensor_scalar_mul(out=gb_cols[:, 2, :], in0=gb_turned[:, 0:GROUPS], scalar1=-1.0)
 
@@ -176,12 +179,9 @@ def tile_yuyipointupdate_pb_kernel(tc, h1, W2, g2, b2, out):
         def statistics(j, b):
             nc.vector.bn_stats(out=stats[:, j, STATS * b : STATS * (b + 1)], in_=z[j, b])
 
-        def make_std(j):
-            nc.vector.bn_aggr(out=mean_var[:, j, :], in_=stats[:, j, :])
-            nc.scalar.activation(out=std[:, j : j + 1], in_=mean_var[:, j, 1:2], func=ACT.Sqrt, bias=EPS_BN)
-
         def make_rstd(j):
-            nc.vector.reciprocal(out=rstd[:, j : j + 1], in_=std[:, j : j + 1])
+            nc.vector.bn_aggr(out=mean_var[:, j, :], in_=stats[:, j, :])
+            nc.scalar.activation(out=rstd[:, j : j + 1], in_=mean_var[:, j, 1:2], func=ACT.Abs_reciprocal_sqrt, bias=EPS_BN)
 
         def make_gain(j):
             nc.scalar.activation(out=gain[:, j, :], in_=gb_cols[:, 0:3:2, j], func=ACT.Identity, scale=rstd[:, j : j + 1])
@@ -226,94 +226,79 @@ def tile_yuyipointupdate_pb_kernel(tc, h1, W2, g2, b2, out):
             nc.scalar.copy(out=rows[:], in_=r_turned[s][:])
             nc.sync.dma_start(out=out[b, :, j * P : (j + 1) * P].rearrange("(t p) o -> p t o", p=P), in_=rows[:])
 
-        turn_w(0)
-        interleave_h(0)
-        group_w(0)
-        interleave_h(1)
-        quantize_h(0)
-        quantize_w(0)
-        interleave_h(2)
-        quantize_h(1)
-        turn_w(PARKED)
-        group_w(PARKED)
-        turn_g2_b2()
-        matmul(0, 0)
-        interleave_h(3)
-        quantize_h(2)
-        quantize_w(PARKED)
-        matmul_pass(0, 1, 0)
-        statistics(0, 0)
-        interleave_h(4)
-        quantize_h(3)
-        matmul_pass(0, 1, 1)
-        matmul(PARKED, 0)
-        matmul(PARKED, 1)
-        interleave_h(5)
-        quantize_h(4)
-        turn_w(1)
-        matmul_pass(0, 2, 0)
-        statistics(0, 1)
-        interleave_h(6)
-        quantize_h(5)
-        turn_w(3)
-        matmul_pass(0, 2, 1)
-        interleave_h(7)
-        quantize_h(6)
-        matmul_pass(0, 3, 0)
-        statistics(0, 2)
-        group_w(1)
-        group_w(3)
-        matmul(PARKED, 2)
-        quantize_h(7)
-        matmul_pass(0, 3, 1)
-        matmul(PARKED, 3)
-
         engines = {mybir.EngineType.DVE, mybir.EngineType.Activation, mybir.EngineType.PE}
         with tc.manual_schedule(engines=engines):
+            turn_w(0)
+            interleave_h(0)
+            group_w(0)
+            quantize_h(0)
+            interleave_h(1)
+            quantize_w(0)
+            matmul_pass(0, 0, 0)
+            for i in range(1, CHUNKS):
+                b, g = divmod(i, PASSES)
+                if i + 1 < CHUNKS:
+                    interleave_h(i + 1)
+                if i == 2:
+                    group_w(PARKED)
+                if i == 3:
+                    quantize_w(PARKED)
+                if i == CHUNKS - 1:
+                    group_w(1)
+                    group_w(3)
+                    matmul(PARKED, b - 1)
+                    matmul_pass(PARKED, b, 0)
+                quantize_h(i)
+                if i == 1:
+                    turn_w(PARKED)
+                    turn_g2_b2()
+                if i == 2:
+                    spread_g2_b2()
+                if i == 3:
+                    matmul(PARKED, 0)
+                if i == 4:
+                    turn_w(1)
+                if i == 5:
+                    turn_w(3)
+                matmul_pass(0, b, g)
+                if i == 3:
+                    matmul(PARKED, 1)
+                if g == 0:
+                    statistics(0, b - 1)
+            matmul_pass(PARKED, B - 1, 1)
+
             quantize_w(1)
             quantize_w(3)
-            park(0)
-            park(1)
-            statistics(0, 3)
-            park(2)
-            make_std(0)
-            matmul(1, 0)
-            matmul(1, 1)
-            park(3)
-            statistics(1, 0)
+            for b in range(B):
+                park(b)
+            statistics(0, B - 1)
             make_rstd(0)
             make_gain(0)
             make_shift(0)
-            matmul(1, 2)
-            matmul(1, 3)
-            for b in range(1, B):
+            for b in range(B):
+                matmul(1, b)
                 statistics(1, b)
 
-            on_vector = (10, 11, 13, 15)
-            stats_done = {0: 1, B: PARKED, 2 * B: 3}
             for s in range(B - 1):
                 normalise_on_scalar(s)
             for s in range(TILES + LAG):
-                if s + 1 in on_vector:
+                if s + 1 in ON_VECTOR:
                     normalise_on_vector(s + 1)
-                if s > LAG:
-                    store(s - LAG)
+                if s - 1 in STATS_DONE:
+                    make_gain(STATS_DONE[s - 1])
+                if s == 1 or s > LAG:
+                    store(max(s - LAG, 0))
+                if s - 1 in STATS_DONE:
+                    make_shift(STATS_DONE[s - 1])
                 if s < TILES:
                     leaky_relu(s)
                     turn_r(s)
                 if s == 0:
                     normalise_on_scalar(B - 1)
-                if s in stats_done:
-                    make_std(stats_done[s])
-                if s - 1 in stats_done:
-                    make_rstd(stats_done[s - 1])
-                    make_gain(stats_done[s - 1])
-                if s == 1:
-                    store(0)
-                if s - 1 in stats_done:
-                    make_shift(stats_done[s - 1])
-                if B <= s + LEAD < TILES and s + LEAD not in on_vector:
+                if B <= s + LEAD < TILES and s + LEAD not in ON_VECTOR:
                     normalise_on_scalar(s + LEAD)
+                if s in STATS_DONE:
+                    make_rstd(STATS_DONE[s])
                 if s < B:
                     matmul(3, s)
                 if s < 2 * B:

@@ -77,6 +77,9 @@ def tile_yuyipointupdate_pb_kernel(tc, h1, W2, g2, b2, out):
         make_identity(nc, ident[:])
         make_identity(nc, ident_bf16[:])
         nc.gpsimd.memset(gb_rows[:], 0.0)
+        table_warm_up = keep.tile([P, 1], F32)
+        nc.vector.memset(table_warm_up[:], 1.0)
+        nc.scalar.activation(out=table_warm_up[:], in_=table_warm_up[:], func=ACT.Abs_reciprocal_sqrt)
 
         def load_h(i, nodes=slice(0, N)):
             b, g = divmod(i, PASSES)

from contextlib import ExitStack

import concourse.mybir as mybir
from concourse.masks import make_identity

B, N, D = 4, 512, 512
C = 2 * D
EPS_BN = 1e-5
NEG_SLOPE = 0.01
FLOPS = 2 * B * N * D * C

F32 = mybir.dt.float32
BF16 = mybir.dt.bfloat16
U32 = mybir.dt.uint32
U8 = mybir.dt.uint8
E5M2X4 = mybir.dt.float8_e5m2_x4
ALU = mybir.AluOpType
ACT = mybir.ActivationFunctionType

P = 128
PACK = 4
K_PASS = P * PACK
PASSES = C // K_PASS
CHUNKS = B * PASSES
GROUPS = D // P
N_TILES = N // P
TILES = GROUPS * B
STATS = 6
RUN = 4

VECTOR_NODES = 208
FIRST_VECTOR_NODES = 424

PARKED = 2
LEAD = 2
LAG = 2
STATS_DONE = {0: 1, B: PARKED, 2 * B: 3}
ON_VECTOR = (PARKED * B + 2, PARKED * B + 3, TILES - 3, TILES - 1)


def z_bank(j, b):
    return {0: b, 1: B + b, PARKED: B + b, 3: LEAD + b}[j]


def turned_bank(j, b):
    if j == GROUPS - 1:
        return z_bank(j, b)
    return b % 2 if j == 0 or b < 2 else B + b


def tile_yuyipointupdate_pb_kernel(tc, h1, W2, g2, b2, out):
    nc = tc.nc

    with ExitStack() as ctx:
        keep = ctx.enter_context(tc.tile_pool(name="keep", bufs=1))
        stage = ctx.enter_context(tc.tile_pool(name="stage", bufs=3))
        post = ctx.enter_context(tc.tile_pool(name="post", bufs=6))
        psum = ctx.enter_context(tc.psum_pool(name="psum", bufs=1))

        ident = keep.tile([P, P], F32)
        ident_bf16 = keep.tile([P, P], BF16)
        gb_rows = keep.tile([P, P], BF16)
        gb_cols = keep.tile([P, 3, GROUPS], F32)
        h_raw = keep.tile([P, CHUNKS, PACK, N], BF16)
        w_raw = keep.tile([P, GROUPS, C], BF16)
        h_codes = keep.tile([P, CHUNKS, N], U32, align_bytes=64)
        h_scales = keep.tile([P, CHUNKS, N], U8, align_bytes=64)
        w_codes = keep.tile([P, GROUPS, PASSES * P], U32, align_bytes=64)
        w_scales = keep.tile([P, GROUPS, PASSES * P], U8, align_bytes=64)
        parked = keep.tile([P, B, N], F32)
        stats = keep.tile([P, GROUPS, B * STATS], F32)
        mean_var = keep.tile([P, GROUPS, 2], F32)
        rstd = keep.tile([P, GROUPS], F32)
        gain = keep.tile([P, GROUPS, 2], F32)
        shift = keep.tile([P, GROUPS], F32)

        make_identity(nc, ident[:])
        make_identity(nc, ident_bf16[:])
        nc.gpsimd.memset(gb_rows[:], 0.0)
        table_warm_up = keep.tile([P, 1], F32)
        nc.vector.memset(table_warm_up[:], 1.0)
        nc.scalar.activation(out=table_warm_up[:], in_=table_warm_up[:], func=ACT.Abs_reciprocal_sqrt)

        def load_h(i, nodes=slice(0, N)):
            b, g = divmod(i, PASSES)
            rows = h1[b, g * K_PASS : (g + 1) * K_PASS, nodes]
            nc.sync.dma_start(out=h_raw[:, i, :, nodes], in_=rows.rearrange("(p t) n -> p t n", t=PACK))

        def load_w(j):
            nc.sync.dma_start(out=w_raw[:, j, :], in_=W2[j * P : (j + 1) * P, :])

        load_w(0)
        load_h(0, slice(0, N // 2))
        load_h(0, slice(N // 2, N))
        load_h(1)
        load_h(2)
        load_w(PARKED)
        nc.sync.dma_start(out=gb_rows[0:GROUPS, :], in_=g2.rearrange("(j p) -> j p", p=P))
        nc.sync.dma_start(out=gb_rows[GROUPS : 2 * GROUPS, :], in_=b2.rearrange("(j p) -> j p", p=P))
        for i in range(3, CHUNKS - 1):
            load_h(i)
        load_w(1)
        load_h(CHUNKS - 1)
        load_w(3)

        def bank_tile(bank, shape, dtype):
            return psum.tile(shape, dtype, name="bank%d" % bank, tag="bank%d" % bank)

        gb_turned = bank_tile(z_bank(0, B - 1), [P, P], BF16)
        h_grouped, w_turned, w_grouped, z, y, r, r_turned = {}, {}, {}, {}, {}, {}, {}

        def interleave_h(i):
            h_grouped[i] = stage.tile([P, N, PACK], BF16, name="h_grouped", align_bytes=64)
            if i == 0:
                shares = [
                    (nc.vector.tensor_copy, slice(0, N // 2)),
                    (nc.vector.tensor_copy, slice(N // 2, FIRST_VECTOR_NODES)),
                    (nc.scalar.copy, slice(FIRST_VECTOR_NODES, N)),
                ]
            else:
                shares = [(nc.vector.tensor_copy, slice(0, VECTOR_NODES)), (nc.scalar.copy, slice(VECTOR_NODES, N))]
            for copy, nodes in shares:
                copy(
                    out=h_grouped[i][:, nodes, :].rearrange("p (c i) t -> p c t i", i=RUN),
                    in_=h_raw[:, i, :, nodes].rearrange("p t (c i) -> p c t i", i=RUN),
                )

        def quantize_h(i):
            nc.vector.quantize_mx(
                out=h_codes[:, i, :].bitcast(E5M2X4),
                scales=h_scales[:, i, :],
                in_=h_grouped[i][:].rearrange("p n t -> p (n t)"),
            )

        def turn_w(j):
            words = w_raw[:, j, :].bitcast(F32)
            w_turned[j] = bank_tile(z_bank(PARKED, 2 + j // 2), [P, 2 * PASSES, P], F32)
            half = K_PASS // 2
            for g in range(PASSES):
                for u in range(2):
                    nc.tensor.transpose(w_turned[j][:, 2 * g + u, :], words[:, half * g + u : half * (g + 1) : 2], ident[:])

        def group_w(j):
            w_grouped[j] = stage.tile([P, C], BF16, name="w_grouped", bufs=GROUPS, align_bytes=64)
            nc.scalar.copy(
                out=w_grouped[j][:].bitcast(F32).rearrange("p (g o u) -> p g o u", g=PASSES, u=2),
                in_=w_turned[j][:].rearrange("p (g u) o -> p g o u", u=2),
            )

        def quantize_w(j):
            nc.vector.quantize_mx(out=w_codes[:, j, :].bitcast(E5M2X4), scales=w_scales[:, j, :], in_=w_grouped[j][:])

        def turn_g2_b2():
            nc.tensor.transpose(gb_turned[:], gb_rows[:], ident_bf16[:])

        def spread_g2_b2():
            nc.vector.tensor_copy(out=gb_cols[:, 0:2, :].rearrange("p a j -> p (a j)"), in_=gb_turned[:, 0 : 2 * GROUPS])
            nc.vector.tensor_scalar_mul(out=gb_cols[:, 2, :], in0=gb_turned[:, 0:GROUPS], scalar1=-1.0)

        def matmul_pass(j, b, g):
            if g == 0:
                z[j, b] = bank_tile(z_bank(j, b), [P, N], F32)[:]
            cols = slice(g * P, (g + 1) * P)
            nc.tensor.matmul_mx(
                out=z[j, b],
                lhsT=w_codes[:, j, cols].bitcast(E5M2X4),
                lhsT_scale=w_scales[:, j, cols],
                rhs=h_codes[:, PASSES * b + g, :].bitcast(E5M2X4),
                rhs_scale=h_scales[:, PASSES * b + g, :],
                start=(g == 0),
                stop=(g == PASSES - 1),
            )

        def matmul(j, b):
            for g in range(PASSES):
                matmul_pass(j, b, g)

        def park(b):
            nc.scalar.copy(out=parked[:, b, :], in_=z[PARKED, b])
            z[PARKED, b] = parked[:, b, :]

        def statistics(j, b):
            nc.vector.bn_stats(out=stats[:, j, STATS * b : STATS * (b + 1)], in_=z[j, b])

        def make_rstd(j):
            nc.vector.bn_aggr(out=mean_var[:, j, :], in_=stats[:, j, :])
            nc.scalar.activation(out=rstd[:, j : j + 1], in_=mean_var[:, j, 1:2], func=ACT.Abs_reciprocal_sqrt, bias=EPS_BN)

        def make_gain(j):
            nc.scalar.activation(out=gain[:, j, :], in_=gb_cols[:, 0:3:2, j], func=ACT.Identity, scale=rstd[:, j : j + 1])

        def make_shift(j):
            nc.scalar.activation(
                out=shift[:, j : j + 1],
                in_=mean_var[:, j, 0:1],
                func=ACT.Identity,
                scale=gain[:, j, 1:2],
                bias=gb_cols[:, 1, j : j + 1],
            )

        def normalise_on_scalar(s):
            j, b = divmod(s, B)
            y[s] = post.tile([P, N], F32, name="y")
            nc.scalar.activation(
                out=y[s][:], in_=z[j, b], func=ACT.Identity, scale=gain[:, j, 0:1], bias=shift[:, j : j + 1]
            )

        def normalise_on_vector(s):
            j, b = divmod(s, B)
            y[s] = post.tile([P, N], F32, name="y")
            nc.vector.tensor_scalar(
                out=y[s][:], in0=z[j, b], scalar1=gain[:, j, 0:1], scalar2=shift[:, j : j + 1], op0=ALU.mult, op1=ALU.add
            )

        def leaky_relu(s):
            r[s] = post.tile([P, N], F32, name="r")
            nc.vector.scalar_tensor_tensor(
                out=r[s][:], in0=y[s][:], scalar=NEG_SLOPE, in1=y[s][:], op0=ALU.mult, op1=ALU.max
            )

        def turn_r(s):
            r_turned[s] = bank_tile(turned_bank(*divmod(s, B)), [P, N_TILES, P], F32)
            for t in range(N_TILES):
                nc.tensor.transpose(r_turned[s][:, t, :], r[s][:, t * P : (t + 1) * P], ident[:])

        def store(s):
            j, b = divmod(s, B)
            rows = post.tile([P, N_TILES, P], F32, name="rows", bufs=8)
            nc.scalar.copy(out=rows[:], in_=r_turned[s][:])
            nc.sync.dma_start(out=out[b, :, j * P : (j + 1) * P].rearrange("(t p) o -> p t o", p=P), in_=rows[:])

        engines = {mybir.EngineType.DVE, mybir.EngineType.Activation, mybir.EngineType.PE}
        with tc.manual_schedule(engines=engines):
            turn_w(0)
            interleave_h(0)
            group_w(0)
            quantize_h(0)
            interleave_h(1)
            quantize_w(0)
            matmul_pass(0, 0, 0)
            for i in range(1, CHUNKS):
                b, g = divmod(i, PASSES)
                if i + 1 < CHUNKS:
                    interleave_h(i + 1)
                if i == 2:
                    group_w(PARKED)
                if i == 3:
                    quantize_w(PARKED)
                if i == CHUNKS - 1:
                    group_w(1)
                    group_w(3)
                    matmul(PARKED, b - 1)
                    matmul_pass(PARKED, b, 0)
                quantize_h(i)
                if i == 1:
                    turn_w(PARKED)
                    turn_g2_b2()
                if i == 2:
                    spread_g2_b2()
                if i == 3:
                    matmul(PARKED, 0)
                if i == 4:
                    turn_w(1)
                if i == 5:
                    turn_w(3)
                matmul_pass(0, b, g)
                if i == 3:
                    matmul(PARKED, 1)
                if g == 0:
                    statistics(0, b - 1)
            matmul_pass(PARKED, B - 1, 1)

            quantize_w(1)
            quantize_w(3)
            for b in range(B):
                park(b)
            statistics(0, B - 1)
            make_rstd(0)
            make_gain(0)
            make_shift(0)
            for b in range(B):
                matmul(1, b)
                statistics(1, b)

            for s in range(B - 1):
                normalise_on_scalar(s)
            for s in range(TILES + LAG):
                if s + 1 in ON_VECTOR:
                    normalise_on_vector(s + 1)
                if s - 1 in STATS_DONE:
                    make_gain(STATS_DONE[s - 1])
                if s == 1 or s > LAG:
                    store(max(s - LAG, 0))
                if s - 1 in STATS_DONE:
                    make_shift(STATS_DONE[s - 1])
                if s < TILES:
                    leaky_relu(s)
                    turn_r(s)
                if s == 0:
                    normalise_on_scalar(B - 1)
                if B <= s + LEAD < TILES and s + LEAD not in ON_VECTOR:
                    normalise_on_scalar(s + LEAD)
                if s in STATS_DONE:
                    make_rstd(STATS_DONE[s])
                if s < B:
                    matmul(3, s)
                if s < 2 * B:
                    statistics(PARKED + s // B, s % B)
